import numpy as np
import ml_dtypes


def mxq(x, axis, fmt="e4m3"):
    dtype, down = {"e4m3": (ml_dtypes.float8_e4m3fn, 7), "e5m2": (ml_dtypes.float8_e5m2, 14)}[fmt]
    v = np.moveaxis(np.asarray(x, np.float32).astype(ml_dtypes.bfloat16).astype(np.float64), axis, -1)
    blocks = v.reshape(v.shape[:-1] + (-1, 32))
    amax = np.abs(blocks).max(-1, keepdims=True)
    byte = np.maximum(np.where(amax > 0, np.frexp(amax)[1] - 1 + 127, 0) - down, 1)
    scale = np.exp2(byte - 127.0)
    codes = (blocks / scale).astype(np.float32).astype(dtype).astype(np.float64)
    return np.moveaxis((codes * scale).reshape(v.shape), -1, axis)


WIDE = False


def mx_kscale(k):
    if not WIDE:
        return np.ones(k)
    levels = np.array([20, -20, 10, -10, 0])
    a = np.random.permutation(np.resize(levels, k // 512 * 4)).reshape(k // 512, 4)
    idx = np.arange(k)
    return np.exp2(a[idx // 512, idx % 128 // 32])


BF16 = ml_dtypes.bfloat16


def bf(x):
    return np.asarray(x, np.float32).astype(BF16)


def f64(x):
    return np.asarray(x).astype(np.float64)


T, S, B, E, Z = 512, 512, 2, 1024, 128
N = T * B


def sigmoid(v):
    return 1.0 / (1.0 + np.exp(-v))


def setup_inputs():
    s = mx_kscale(N).reshape(T, B, 1)
    query = bf(np.random.standard_normal((T, B, E)))
    hr0 = bf(np.random.standard_normal((T, B, E)) * 0.2)
    Wu = bf(np.random.standard_normal((E, E)) / np.sqrt(E))
    bu = bf(np.random.standard_normal(E) * 0.3)
    Wh = bf(np.random.standard_normal((E, E)) * 5.0 / np.sqrt(E))
    bh = bf(np.random.standard_normal(E) * 0.3)
    g = bf(np.random.standard_normal((T, B, E)) * np.exp2(np.random.randint(-12, 1, (T, B, 1))) * 4.0 / s)
    u = sigmoid(f64(query) @ f64(Wu).T + f64(bu))
    h = np.tanh(f64(hr0) @ f64(Wh).T + f64(bh))
    return {"query": query, "hr": bf(f64(hr0) * s), "Wu": Wu, "bu": bu, "Wh": Wh, "bh": bh,
            "u": np.asarray(u, np.float32), "h": np.asarray(h, np.float32), "grad_out": g}


def reference(query, hr, Wu, bu, Wh, bh, u, h, grad_out):
    hf = f64(h)
    dz = f64(grad_out) * f64(u) * (1.0 - hf * hf)
    dz2 = dz.reshape(N, E)
    a = f64(hr).reshape(N, E)
    return mxq(dz2, 0, "e5m2").T @ mxq(a, 0, "e4m3")

@@ -1,0 +1,169 @@
+from contextlib import ExitStack
+
+import concourse.mybir as mybir
+
+F32 = mybir.dt.float32
+BF16 = mybir.dt.bfloat16
+U32 = mybir.dt.uint32
+U8 = mybir.dt.uint8
+E4M3_X4 = mybir.dt.float8_e4m3fn_x4
+E5M2_X4 = mybir.dt.float8_e5m2_x4
+ALU = mybir.AluOpType
+ACT = mybir.ActivationFunctionType
+
+P = 128
+PACK = 4
+K_PASS = P * PACK
+TOKENS = 1024
+E = 1024
+PASSES = TOKENS // K_PASS
+M_TILE = 128
+N_TILE = 512
+M_BLOCKS = E // M_TILE
+N_BLOCKS = E // N_TILE
+PSUM_BANKS = 8
+EARLY = PSUM_BANKS // N_BLOCKS
+HALF = PACK // 2
+RUN = 4
+
+FLOPS = 2 * TOKENS * E * E
+BYTES = TOKENS * E * (2 + 2 + 4 + 4) + E * E * 4
+
+
+def by_column(rows_first):
+    return rows_first.rearrange("p j (b i) -> p b j i", i=RUN)
+
+
+def by_column_grouped(grouped):
+    return grouped.rearrange("p (b i) j -> p b j i", i=RUN)
+
+
+def tile_gatedcrossattention_pb_v_kernel(
+    tc, query, hr, Wu, bu, Wh, bh, u, h, grad_out, out
+):
+    nc = tc.nc
+
+    def pass_rows(dram, c):
+        flat = dram.flatten_outer_dims()
+        return flat[c * K_PASS : (c + 1) * K_PASS, :].rearrange("(p j) e -> p j e", j=PACK)
+
+    with ExitStack() as stack:
+        keep = stack.enter_context(tc.tile_pool(name="keep", bufs=1))
+        psum = stack.enter_context(tc.psum_pool(name="psum", bufs=PSUM_BANKS))
+
+        hr_raw = [keep.tile([P, PACK, E], BF16, name="hr_raw%d" % c) for c in range(PASSES)]
+        g_raw = [keep.tile([P, PACK, E], BF16, name="g_raw%d" % c) for c in range(PASSES)]
+        u_raw = [keep.tile([P, PACK, E], F32, name="u_raw%d" % c) for c in range(PASSES)]
+        factor = [keep.tile([P, PACK, E], F32, name="factor%d" % c) for c in range(PASSES)]
+
+        for c in range(PASSES):
+            nc.sync.dma_start(out=hr_raw[c][:], in_=pass_rows(hr, c))
+        for c in range(PASSES):
+            for dst, src in ((factor[c], h), (u_raw[c], u)):
+                for j in range(0, PACK, HALF):
+                    nc.sync.dma_start(
+                        out=dst[:, j : j + HALF, :], in_=pass_rows(src, c)[:, j : j + HALF, :]
+                    )
+            nc.sync.dma_start(out=g_raw[c][:], in_=pass_rows(grad_out, c))
+
+        hr_grouped = [
+            keep.tile([P, E, PACK], BF16, name="hr_grouped%d" % c, align_bytes=64)
+            for c in range(PASSES)
+        ]
+        dz_grouped = [
+            keep.tile([P, E, PACK], BF16, name="dz_grouped%d" % c, align_bytes=64)
+            for c in range(PASSES)
+        ]
+        hr_codes = keep.tile([P, PASSES, E], U32, name="hr_codes", align_bytes=64)
+        hr_scales = keep.tile([P, PASSES, E], U8, name="hr_scales", align_bytes=64)
+        dz_codes = keep.tile([P, PASSES, E], U32, name="dz_codes", align_bytes=64)
+        dz_scales = keep.tile([P, PASSES, E], U8, name="dz_scales", align_bytes=64)
+
+        for c in range(PASSES):
+            nc.vector.tensor_copy(out=by_column_grouped(hr_grouped[c][:]), in_=by_column(hr_raw[c][:]))
+        for c in range(PASSES):
+            nc.vector.quantize_mx(
+                out=hr_codes[:, c, :].bitcast(E4M3_X4),
+                scales=hr_scales[:, c, :],
+                in_=hr_grouped[c][:].rearrange("p e j -> p (e j)"),
+            )
+
+        def gate_times_slope(c):
+            for j in range(0, PACK, HALF):
+                rows = factor[c][:, j : j + HALF, :]
+                nc.scalar.activation(out=rows, in_=rows, func=ACT.Square)
+            for j in range(0, PACK, HALF):
+                rows = factor[c][:, j : j + HALF, :]
+                nc.vector.scalar_tensor_tensor(
+                    out=rows,
+                    in0=rows,
+                    scalar=1.0,
+                    in1=u_raw[c][:, j : j + HALF, :],
+                    op0=ALU.subtract,
+                    op1=ALU.mult,
+                )
+
+        def dz_columns(c, cols):
+            nc.vector.scalar_tensor_tensor(
+                out=dz_grouped[c][:, cols, :],
+                in0=factor[c][:, :, cols].rearrange("p j e -> p e j"),
+                scalar=-1.0,
+                in1=g_raw[c][:, :, cols].rearrange("p j e -> p e j"),
+                op0=ALU.mult,
+                op1=ALU.mult,
+            )
+
+        def quantise_dz(c, cols):
+            nc.vector.quantize_mx(
+                out=dz_codes[:, c, cols].bitcast(E5M2_X4),
+                scales=dz_scales[:, c, cols],
+                in_=dz_grouped[c][:, cols, :].rearrange("p e j -> p (e j)"),
+            )
+
+        sums = {}
+
+        def multiply(c, m):
+            m_cols = slice(m * M_TILE, (m + 1) * M_TILE)
+            for n in range(N_BLOCKS):
+                n_cols = slice(n * N_TILE, (n + 1) * N_TILE)
+                if c == 0:
+                    sums[m, n] = psum.tile([M_TILE, N_TILE], F32, name="sums")
+                nc.tensor.matmul_mx(
+                    out=sums[m, n][:],
+                    lhsT=dz_codes[:, c, m_cols].bitcast(E5M2_X4),
+                    lhsT_scale=dz_scales[:, c, m_cols],
+                    rhs=hr_codes[:, c, n_cols].bitcast(E4M3_X4),
+                    rhs_scale=hr_scales[:, c, n_cols],
+                    start=(c == 0),
+                    stop=(c == PASSES - 1),
+                )
+
+        def store(m):
+            result = keep.tile([M_TILE, E], F32, name="result%d" % m)
+            for n in range(N_BLOCKS):
+                if m % 2 == 1 and n == N_BLOCKS - 1:
+                    nc.vector.tensor_copy(out=result[:, n * N_TILE : (n + 1) * N_TILE], in_=sums[m, n][:])
+                else:
+                    nc.scalar.copy(out=result[:, n * N_TILE : (n + 1) * N_TILE], in_=sums[m, n][:])
+            nc.sync.dma_start(out=out[m * M_TILE : (m + 1) * M_TILE, :], in_=result[:])
+
+        gate_times_slope(0)
+        for n in range(N_BLOCKS):
+            dz_columns(0, slice(n * N_TILE, (n + 1) * N_TILE))
+        for n in range(N_BLOCKS):
+            quantise_dz(0, slice(n * N_TILE, (n + 1) * N_TILE))
+        for m in range(EARLY):
+            multiply(0, m)
+
+        gate_times_slope(1)
+        block = [slice(m * M_TILE, (m + 1) * M_TILE) for m in range(M_BLOCKS)]
+        dz_columns(1, block[0])
+        for m in range(M_BLOCKS):
+            if m + 1 < M_BLOCKS:
+                dz_columns(1, block[m + 1])
+            quantise_dz(1, block[m])
+            multiply(1, m)
+            store(m)
+            ahead = m - 1 + EARLY
+            if m >= 1 and ahead < M_BLOCKS:
+                multiply(0, ahead)

@@ -17,25 +17,19 @@ K_PASS = P * PACK
 TOKENS = 1024
 E = 1024
 PASSES = TOKENS // K_PASS
+LAST = PASSES - 1
 M_TILE = 128
 N_TILE = 512
-M_BLOCKS = E // M_TILE
 N_BLOCKS = E // N_TILE
 PSUM_BANKS = 8
-EARLY = PSUM_BANKS // N_BLOCKS
-HALF = PACK // 2
+ROUND_BLOCKS = PSUM_BANKS // N_BLOCKS
+ROUND_COLS = ROUND_BLOCKS * M_TILE
+ROUNDS = E // ROUND_COLS
+HALF_ROWS = PACK // 2
 RUN = 4
 
 FLOPS = 2 * TOKENS * E * E
 BYTES = TOKENS * E * (2 + 2 + 4 + 4) + E * E * 4
-
-
-def by_column(rows_first):
-    return rows_first.rearrange("p j (b i) -> p b j i", i=RUN)
-
-
-def by_column_grouped(grouped):
-    return grouped.rearrange("p (b i) j -> p b j i", i=RUN)
 
 
 def tile_gatedcrossattention_pb_v_kernel(
@@ -47,9 +41,15 @@ def tile_gatedcrossattention_pb_v_kernel(
         flat = dram.flatten_outer_dims()
         return flat[c * K_PASS : (c + 1) * K_PASS, :].rearrange("(p j) e -> p j e", j=PACK)
 
+    def piece(view, c, k):
+        if c < LAST:
+            return view[:, k * HALF_ROWS : (k + 1) * HALF_ROWS, :]
+        return view[:, :, k * ROUND_COLS : (k + 1) * ROUND_COLS]
+
     with ExitStack() as stack:
         keep = stack.enter_context(tc.tile_pool(name="keep", bufs=1))
         psum = stack.enter_context(tc.psum_pool(name="psum", bufs=PSUM_BANKS))
+        stack.enter_context(tc.manual_schedule())
 
         hr_raw = [keep.tile([P, PACK, E], BF16, name="hr_raw%d" % c) for c in range(PASSES)]
         g_raw = [keep.tile([P, PACK, E], BF16, name="g_raw%d" % c) for c in range(PASSES)]
@@ -58,13 +58,14 @@ def tile_gatedcrossattention_pb_v_kernel(
 
         for c in range(PASSES):
             nc.sync.dma_start(out=hr_raw[c][:], in_=pass_rows(hr, c))
-        for c in range(PASSES):
-            for dst, src in ((factor[c], h), (u_raw[c], u)):
-                for j in range(0, PACK, HALF):
-                    nc.sync.dma_start(
-                        out=dst[:, j : j + HALF, :], in_=pass_rows(src, c)[:, j : j + HALF, :]
-                    )
-            nc.sync.dma_start(out=g_raw[c][:], in_=pass_rows(grad_out, c))
+        for k in range(2):
+            nc.sync.dma_start(out=piece(factor[0], 0, k), in_=piece(pass_rows(h, 0), 0, k))
+        for k in range(2):
+            nc.sync.dma_start(out=piece(u_raw[0], 0, k), in_=piece(pass_rows(u, 0), 0, k))
+        nc.sync.dma_start(out=g_raw[0][:], in_=pass_rows(grad_out, 0))
+        for k in range(ROUNDS):
+            for dst, src in ((factor[LAST], h), (u_raw[LAST], u), (g_raw[LAST], grad_out)):
+                nc.sync.dma_start(out=piece(dst, LAST, k), in_=piece(pass_rows(src, LAST), LAST, k))
 
         hr_grouped = [
             keep.tile([P, E, PACK], BF16, name="hr_grouped%d" % c, align_bytes=64)
@@ -80,7 +81,10 @@ def tile_gatedcrossattention_pb_v_kernel(
         dz_scales = keep.tile([P, PASSES, E], U8, name="dz_scales", align_bytes=64)
 
         for c in range(PASSES):
-            nc.vector.tensor_copy(out=by_column_grouped(hr_grouped[c][:]), in_=by_column(hr_raw[c][:]))
+            nc.vector.tensor_copy(
+                out=hr_grouped[c][:].rearrange("p (b i) j -> p b j i", i=RUN),
+                in_=hr_raw[c][:].rearrange("p j (b i) -> p b j i", i=RUN),
+            )
         for c in range(PASSES):
             nc.vector.quantize_mx(
                 out=hr_codes[:, c, :].bitcast(E4M3_X4),
@@ -88,20 +92,18 @@ def tile_gatedcrossattention_pb_v_kernel(
                 in_=hr_grouped[c][:].rearrange("p e j -> p (e j)"),
             )
 
-        def gate_times_slope(c):
-            for j in range(0, PACK, HALF):
-                rows = factor[c][:, j : j + HALF, :]
-                nc.scalar.activation(out=rows, in_=rows, func=ACT.Square)
-            for j in range(0, PACK, HALF):
-                rows = factor[c][:, j : j + HALF, :]
-                nc.vector.scalar_tensor_tensor(
-                    out=rows,
-                    in0=rows,
-                    scalar=1.0,
-                    in1=u_raw[c][:, j : j + HALF, :],
-                    op0=ALU.subtract,
-                    op1=ALU.mult,
-                )
+        def square(c, k):
+            nc.scalar.activation(out=piece(factor[c], c, k), in_=piece(factor[c], c, k), func=ACT.Square)
+
+        def times_gate(c, k):
+            nc.vector.scalar_tensor_tensor(
+                out=piece(factor[c], c, k),
+                in0=piece(factor[c], c, k),
+                scalar=1.0,
+                in1=piece(u_raw[c], c, k),
+                op0=ALU.subtract,
+                op1=ALU.mult,
+            )
 
         def dz_columns(c, cols):
             nc.vector.scalar_tensor_tensor(
@@ -135,35 +137,35 @@ def tile_gatedcrossattention_pb_v_kernel(
                     rhs=hr_codes[:, c, n_cols].bitcast(E4M3_X4),
                     rhs_scale=hr_scales[:, c, n_cols],
                     start=(c == 0),
-                    stop=(c == PASSES - 1),
+                    stop=(c == LAST),
                 )
 
-        def store(m):
+        def finish(m):
+            quantise_dz(LAST, slice(m * M_TILE, (m + 1) * M_TILE))
+            multiply(LAST, m)
             result = keep.tile([M_TILE, E], F32, name="result%d" % m)
             for n in range(N_BLOCKS):
-                if m % 2 == 1 and n == N_BLOCKS - 1:
-                    nc.vector.tensor_copy(out=result[:, n * N_TILE : (n + 1) * N_TILE], in_=sums[m, n][:])
-                else:
-                    nc.scalar.copy(out=result[:, n * N_TILE : (n + 1) * N_TILE], in_=sums[m, n][:])
+                nc.scalar.copy(out=result[:, n * N_TILE : (n + 1) * N_TILE], in_=sums[m, n][:])
             nc.sync.dma_start(out=out[m * M_TILE : (m + 1) * M_TILE, :], in_=result[:])
 
-        gate_times_slope(0)
-        for n in range(N_BLOCKS):
-            dz_columns(0, slice(n * N_TILE, (n + 1) * N_TILE))
-        for n in range(N_BLOCKS):
-            quantise_dz(0, slice(n * N_TILE, (n + 1) * N_TILE))
-        for m in range(EARLY):
-            multiply(0, m)
+        for k in range(2):
+            square(0, k)
+        for k in range(2):
+            times_gate(0, k)
+        for k in range(ROUNDS):
+            dz_columns(0, slice(k * ROUND_COLS, (k + 1) * ROUND_COLS))
+        for k in range(ROUNDS):
+            quantise_dz(0, slice(k * ROUND_COLS, (k + 1) * ROUND_COLS))
 
-        gate_times_slope(1)
-        block = [slice(m * M_TILE, (m + 1) * M_TILE) for m in range(M_BLOCKS)]
-        dz_columns(1, block[0])
-        for m in range(M_BLOCKS):
-            if m + 1 < M_BLOCKS:
-                dz_columns(1, block[m + 1])
-            quantise_dz(1, block[m])
-            multiply(1, m)
-            store(m)
-            ahead = m - 1 + EARLY
-            if m >= 1 and ahead < M_BLOCKS:
-                multiply(0, ahead)
+        for k in range(ROUNDS):
+            square(LAST, k)
+        for k in range(ROUNDS):
+            times_gate(LAST, k)
+            blocks = range(k * ROUND_BLOCKS, (k + 1) * ROUND_BLOCKS)
+            for m in blocks:
+                multiply(0, m)
+            for m in blocks:
+                dz_columns(LAST, slice(m * M_TILE, (m + 1) * M_TILE))
+                if m > blocks[0]:
+                    finish(m - 1)
+            finish(blocks[-1])

@@ -25,7 +25,6 @@ PSUM_BANKS = 8
 ROUND_BLOCKS = PSUM_BANKS // N_BLOCKS
 ROUND_COLS = ROUND_BLOCKS * M_TILE
 ROUNDS = E // ROUND_COLS
-HALF_ROWS = PACK // 2
 RUN = 4
 
 FLOPS = 2 * TOKENS * E * E
@@ -42,8 +41,6 @@ def tile_gatedcrossattention_pb_v_kernel(
         return flat[c * K_PASS : (c + 1) * K_PASS, :].rearrange("(p j) e -> p j e", j=PACK)
 
     def piece(view, c, k):
-        if c < LAST:
-            return view[:, k * HALF_ROWS : (k + 1) * HALF_ROWS, :]
         return view[:, :, k * ROUND_COLS : (k + 1) * ROUND_COLS]
 
     with ExitStack() as stack:
@@ -58,14 +55,10 @@ def tile_gatedcrossattention_pb_v_kernel(
 
         for c in range(PASSES):
             nc.sync.dma_start(out=hr_raw[c][:], in_=pass_rows(hr, c))
-        for k in range(2):
-            nc.sync.dma_start(out=piece(factor[0], 0, k), in_=piece(pass_rows(h, 0), 0, k))
-        for k in range(2):
-            nc.sync.dma_start(out=piece(u_raw[0], 0, k), in_=piece(pass_rows(u, 0), 0, k))
-        nc.sync.dma_start(out=g_raw[0][:], in_=pass_rows(grad_out, 0))
-        for k in range(ROUNDS):
-            for dst, src in ((factor[LAST], h), (u_raw[LAST], u), (g_raw[LAST], grad_out)):
-                nc.sync.dma_start(out=piece(dst, LAST, k), in_=piece(pass_rows(src, LAST), LAST, k))
+        for c in range(PASSES):
+            for k in range(ROUNDS):
+                for dst, src in ((factor[c], h), (u_raw[c], u), (g_raw[c], grad_out)):
+                    nc.sync.dma_start(out=piece(dst, c, k), in_=piece(pass_rows(src, c), c, k))
 
         hr_grouped = [
             keep.tile([P, E, PACK], BF16, name="hr_grouped%d" % c, align_bytes=64)
@@ -148,19 +141,21 @@ def tile_gatedcrossattention_pb_v_kernel(
                 nc.scalar.copy(out=result[:, n * N_TILE : (n + 1) * N_TILE], in_=sums[m, n][:])
             nc.sync.dma_start(out=out[m * M_TILE : (m + 1) * M_TILE, :], in_=result[:])
 
-        for k in range(2):
+        halves = [slice(k * ROUND_COLS, (k + 1) * ROUND_COLS) for k in range(ROUNDS)]
+        for k in range(ROUNDS):
             square(0, k)
-        for k in range(2):
-            times_gate(0, k)
-        for k in range(ROUNDS):
-            dz_columns(0, slice(k * ROUND_COLS, (k + 1) * ROUND_COLS))
-        for k in range(ROUNDS):
-            quantise_dz(0, slice(k * ROUND_COLS, (k + 1) * ROUND_COLS))
+        times_gate(0, 0)
+        dz_columns(0, halves[0])
+        times_gate(0, 1)
+        quantise_dz(0, halves[0])
+        dz_columns(0, halves[1])
 
         for k in range(ROUNDS):
             square(LAST, k)
         for k in range(ROUNDS):
             times_gate(LAST, k)
+            if k == 0:
+                quantise_dz(0, halves[1])
             blocks = range(k * ROUND_BLOCKS, (k + 1) * ROUND_BLOCKS)
             for m in blocks:
                 multiply(0, m)

@@ -22,10 +22,11 @@ M_TILE = 128
 N_TILE = 512
 N_BLOCKS = E // N_TILE
 PSUM_BANKS = 8
-ROUND_BLOCKS = PSUM_BANKS // N_BLOCKS
-ROUND_COLS = ROUND_BLOCKS * M_TILE
-ROUNDS = E // ROUND_COLS
+CHUNK_BLOCKS = 2
+CHUNK_COLS = CHUNK_BLOCKS * M_TILE
+CHUNKS = E // CHUNK_COLS
 RUN = 4
+VECTOR_HR_COLS = 704
 
 FLOPS = 2 * TOKENS * E * E
 BYTES = TOKENS * E * (2 + 2 + 4 + 4) + E * E * 4
@@ -40,8 +41,14 @@ def tile_gatedcrossattention_pb_v_kernel(
         flat = dram.flatten_outer_dims()
         return flat[c * K_PASS : (c + 1) * K_PASS, :].rearrange("(p j) e -> p j e", j=PACK)
 
-    def piece(view, c, k):
-        return view[:, :, k * ROUND_COLS : (k + 1) * ROUND_COLS]
+    def chunk_cols(q):
+        return slice(q * CHUNK_COLS, (q + 1) * CHUNK_COLS)
+
+    def block_cols(m):
+        return slice(m * M_TILE, (m + 1) * M_TILE)
+
+    def chunk_blocks(q):
+        return range(q * CHUNK_BLOCKS, (q + 1) * CHUNK_BLOCKS)
 
     with ExitStack() as stack:
         keep = stack.enter_context(tc.tile_pool(name="keep", bufs=1))
@@ -55,10 +62,12 @@ def tile_gatedcrossattention_pb_v_kernel(
 
         for c in range(PASSES):
             nc.sync.dma_start(out=hr_raw[c][:], in_=pass_rows(hr, c))
-        for c in range(PASSES):
-            for k in range(ROUNDS):
+        for q in range(CHUNKS):
+            for c in range(PASSES):
                 for dst, src in ((factor[c], h), (u_raw[c], u), (g_raw[c], grad_out)):
-                    nc.sync.dma_start(out=piece(dst, c, k), in_=piece(pass_rows(src, c), c, k))
+                    nc.sync.dma_start(
+                        out=dst[:, :, chunk_cols(q)], in_=pass_rows(src, c)[:, :, chunk_cols(q)]
+                    )
 
         hr_grouped = [
             keep.tile([P, E, PACK], BF16, name="hr_grouped%d" % c, align_bytes=64)
@@ -73,27 +82,29 @@ def tile_gatedcrossattention_pb_v_kernel(
         dz_codes = keep.tile([P, PASSES, E], U32, name="dz_codes", align_bytes=64)
         dz_scales = keep.tile([P, PASSES, E], U8, name="dz_scales", align_bytes=64)
 
-        for c in range(PASSES):
-            nc.vector.tensor_copy(
-                out=hr_grouped[c][:].rearrange("p (b i) j -> p b j i", i=RUN),
-                in_=hr_raw[c][:].rearrange("p j (b i) -> p b j i", i=RUN),
+        def regroup_hr(copy, c, cols):
+            copy(
+                out=hr_grouped[c][:, cols, :].rearrange("p (b i) j -> p b j i", i=RUN),
+                in_=hr_raw[c][:, :, cols].rearrange("p j (b i) -> p b j i", i=RUN),
             )
-        for c in range(PASSES):
+
+        def quantise_hr(c):
             nc.vector.quantize_mx(
                 out=hr_codes[:, c, :].bitcast(E4M3_X4),
                 scales=hr_scales[:, c, :],
                 in_=hr_grouped[c][:].rearrange("p e j -> p (e j)"),
             )
 
-        def square(c, k):
-            nc.scalar.activation(out=piece(factor[c], c, k), in_=piece(factor[c], c, k), func=ACT.Square)
+        def square(c, q):
+            view = factor[c][:, :, chunk_cols(q)]
+            nc.scalar.activation(out=view, in_=view, func=ACT.Square)
 
-        def times_gate(c, k):
+        def times_gate(c, q):
             nc.vector.scalar_tensor_tensor(
-                out=piece(factor[c], c, k),
-                in0=piece(factor[c], c, k),
+                out=factor[c][:, :, chunk_cols(q)],
+                in0=factor[c][:, :, chunk_cols(q)],
                 scalar=1.0,
-                in1=piece(u_raw[c], c, k),
+                in1=u_raw[c][:, :, chunk_cols(q)],
                 op0=ALU.subtract,
                 op1=ALU.mult,
             )
@@ -116,51 +127,64 @@ def tile_gatedcrossattention_pb_v_kernel(
             )
 
         sums = {}
+        results = {}
 
         def multiply(c, m):
-            m_cols = slice(m * M_TILE, (m + 1) * M_TILE)
             for n in range(N_BLOCKS):
                 n_cols = slice(n * N_TILE, (n + 1) * N_TILE)
                 if c == 0:
                     sums[m, n] = psum.tile([M_TILE, N_TILE], F32, name="sums")
                 nc.tensor.matmul_mx(
                     out=sums[m, n][:],
-                    lhsT=dz_codes[:, c, m_cols].bitcast(E5M2_X4),
-                    lhsT_scale=dz_scales[:, c, m_cols],
+                    lhsT=dz_codes[:, c, block_cols(m)].bitcast(E5M2_X4),
+                    lhsT_scale=dz_scales[:, c, block_cols(m)],
                     rhs=hr_codes[:, c, n_cols].bitcast(E4M3_X4),
                     rhs_scale=hr_scales[:, c, n_cols],
                     start=(c == 0),
                     stop=(c == LAST),
                 )
 
-        def finish(m):
-            quantise_dz(LAST, slice(m * M_TILE, (m + 1) * M_TILE))
-            multiply(LAST, m)
-            result = keep.tile([M_TILE, E], F32, name="result%d" % m)
+        def store(m, copies):
+            results[m] = keep.tile([M_TILE, E], F32, name="result%d" % m)
             for n in range(N_BLOCKS):
-                nc.scalar.copy(out=result[:, n * N_TILE : (n + 1) * N_TILE], in_=sums[m, n][:])
-            nc.sync.dma_start(out=out[m * M_TILE : (m + 1) * M_TILE, :], in_=result[:])
+                copies[n](out=results[m][:, n * N_TILE : (n + 1) * N_TILE], in_=sums[m, n][:])
+            nc.sync.dma_start(out=out[block_cols(m), :], in_=results[m][:])
 
-        halves = [slice(k * ROUND_COLS, (k + 1) * ROUND_COLS) for k in range(ROUNDS)]
-        for k in range(ROUNDS):
-            square(0, k)
-        times_gate(0, 0)
-        dz_columns(0, halves[0])
-        times_gate(0, 1)
-        quantise_dz(0, halves[0])
-        dz_columns(0, halves[1])
+        scalar_alone = (nc.scalar.copy, nc.scalar.copy)
+        both = (nc.scalar.copy, nc.vector.tensor_copy)
 
-        for k in range(ROUNDS):
-            square(LAST, k)
-        for k in range(ROUNDS):
-            times_gate(LAST, k)
-            if k == 0:
-                quantise_dz(0, halves[1])
-            blocks = range(k * ROUND_BLOCKS, (k + 1) * ROUND_BLOCKS)
-            for m in blocks:
+        for c in range(PASSES):
+            regroup_hr(nc.vector.tensor_copy, c, slice(0, VECTOR_HR_COLS))
+            regroup_hr(nc.scalar.copy, c, slice(VECTOR_HR_COLS, E))
+        quantise_hr(0)
+
+        for q in range(CHUNKS):
+            square(0, q)
+            if q >= 2:
+                store(chunk_blocks(q - 2)[1], scalar_alone)
+            times_gate(0, q)
+            if q >= 1:
+                quantise_dz(LAST, chunk_cols(q - 1))
+                for m in chunk_blocks(q - 1):
+                    multiply(LAST, m)
+            dz_columns(0, chunk_cols(q))
+            square(LAST, q)
+            if q >= 1:
+                store(chunk_blocks(q - 1)[0], scalar_alone)
+            times_gate(LAST, q)
+            if q == 0:
+                quantise_hr(LAST)
+            quantise_dz(0, chunk_cols(q))
+            for m in chunk_blocks(q):
                 multiply(0, m)
-            for m in blocks:
-                dz_columns(LAST, slice(m * M_TILE, (m + 1) * M_TILE))
-                if m > blocks[0]:
-                    finish(m - 1)
-            finish(blocks[-1])
+            if q < CHUNKS - 1:
+                dz_columns(LAST, chunk_cols(q))
+
+        for m in chunk_blocks(CHUNKS - 1):
+            dz_columns(LAST, block_cols(m))
+        store(chunk_blocks(CHUNKS - 2)[1], scalar_alone)
+        for m in chunk_blocks(CHUNKS - 1):
+            quantise_dz(LAST, block_cols(m))
+            multiply(LAST, m)
+        for m in chunk_blocks(CHUNKS - 1):
+            store(m, both)

@@ -22,11 +22,10 @@ M_TILE = 128
 N_TILE = 512
 N_BLOCKS = E // N_TILE
 PSUM_BANKS = 8
-CHUNK_BLOCKS = 2
+CHUNK_BLOCKS = 4
 CHUNK_COLS = CHUNK_BLOCKS * M_TILE
 CHUNKS = E // CHUNK_COLS
 RUN = 4
-VECTOR_HR_COLS = 704
 
 FLOPS = 2 * TOKENS * E * E
 BYTES = TOKENS * E * (2 + 2 + 4 + 4) + E * E * 4
@@ -44,8 +43,8 @@ def tile_gatedcrossattention_pb_v_kernel(
     def chunk_cols(q):
         return slice(q * CHUNK_COLS, (q + 1) * CHUNK_COLS)
 
-    def block_cols(m):
-        return slice(m * M_TILE, (m + 1) * M_TILE)
+    def block_cols(m, count=1):
+        return slice(m * M_TILE, (m + count) * M_TILE)
 
     def chunk_blocks(q):
         return range(q * CHUNK_BLOCKS, (q + 1) * CHUNK_BLOCKS)
@@ -99,12 +98,12 @@ def tile_gatedcrossattention_pb_v_kernel(
             view = factor[c][:, :, chunk_cols(q)]
             nc.scalar.activation(out=view, in_=view, func=ACT.Square)
 
-        def times_gate(c, q):
+        def times_gate(c, cols):
             nc.vector.scalar_tensor_tensor(
-                out=factor[c][:, :, chunk_cols(q)],
-                in0=factor[c][:, :, chunk_cols(q)],
+                out=factor[c][:, :, cols],
+                in0=factor[c][:, :, cols],
                 scalar=1.0,
-                in1=u_raw[c][:, :, chunk_cols(q)],
+                in1=u_raw[c][:, :, cols],
                 op0=ALU.subtract,
                 op1=ALU.mult,
             )
@@ -154,37 +153,58 @@ def tile_gatedcrossattention_pb_v_kernel(
         both = (nc.scalar.copy, nc.vector.tensor_copy)
 
         for c in range(PASSES):
-            regroup_hr(nc.vector.tensor_copy, c, slice(0, VECTOR_HR_COLS))
-            regroup_hr(nc.scalar.copy, c, slice(VECTOR_HR_COLS, E))
+            regroup_hr(nc.vector.tensor_copy, c, slice(0, E))
         quantise_hr(0)
 
-        for q in range(CHUNKS):
-            square(0, q)
-            if q >= 2:
-                store(chunk_blocks(q - 2)[1], scalar_alone)
-            times_gate(0, q)
-            if q >= 1:
-                quantise_dz(LAST, chunk_cols(q - 1))
-                for m in chunk_blocks(q - 1):
-                    multiply(LAST, m)
-            dz_columns(0, chunk_cols(q))
-            square(LAST, q)
-            if q >= 1:
-                store(chunk_blocks(q - 1)[0], scalar_alone)
-            times_gate(LAST, q)
-            if q == 0:
-                quantise_hr(LAST)
-            quantise_dz(0, chunk_cols(q))
-            for m in chunk_blocks(q):
-                multiply(0, m)
-            if q < CHUNKS - 1:
-                dz_columns(LAST, chunk_cols(q))
-
-        for m in chunk_blocks(CHUNKS - 1):
-            dz_columns(LAST, block_cols(m))
-        store(chunk_blocks(CHUNKS - 2)[1], scalar_alone)
-        for m in chunk_blocks(CHUNKS - 1):
+        def close(m):
             quantise_dz(LAST, block_cols(m))
             multiply(LAST, m)
-        for m in chunk_blocks(CHUNKS - 1):
-            store(m, both)
+
+        for q in range(CHUNKS):
+            first = q * CHUNK_BLOCKS
+            final = q == CHUNKS - 1
+            if q == 0:
+                square(0, q)
+                square(LAST, q)
+            for pair in (first, first + 2):
+                times_gate(0, block_cols(pair, 2))
+            if q > 0:
+                close(first - 1)
+                store(first - 2, scalar_alone)
+                store(first - 1, scalar_alone)
+            for pair in (first, first + 2):
+                dz_columns(0, block_cols(pair, 2))
+            quantise_dz(0, block_cols(first, 2))
+            if q == 0:
+                quantise_hr(LAST)
+            else:
+                times_gate(LAST, block_cols(first, 2))
+            quantise_dz(0, block_cols(first + 2, 2))
+            for m in chunk_blocks(q):
+                multiply(0, m)
+            if q == 0:
+                times_gate(LAST, block_cols(first, 2))
+                times_gate(LAST, block_cols(first + 2, 2))
+            dz_columns(LAST, block_cols(first))
+            dz_columns(LAST, block_cols(first + 1))
+            close(first)
+            if final:
+                times_gate(LAST, block_cols(first + 2, 2))
+                close(first + 1)
+                dz_columns(LAST, block_cols(first + 2))
+                dz_columns(LAST, block_cols(first + 3))
+                close(first + 2)
+                close(first + 3)
+                store(first, scalar_alone)
+                store(first + 1, scalar_alone)
+                store(first + 2, both)
+                store(first + 3, both)
+            else:
+                dz_columns(LAST, block_cols(first + 2))
+                close(first + 1)
+                dz_columns(LAST, block_cols(first + 3))
+                close(first + 2)
+                square(0, q + 1)
+                store(first, scalar_alone)
+                store(first + 1, scalar_alone)
+                square(LAST, q + 1)

@@ -26,6 +26,7 @@ CHUNK_BLOCKS = 4
 CHUNK_COLS = CHUNK_BLOCKS * M_TILE
 CHUNKS = E // CHUNK_COLS
 RUN = 4
+VECTOR_HR_COLS = 704
 
 FLOPS = 2 * TOKENS * E * E
 BYTES = TOKENS * E * (2 + 2 + 4 + 4) + E * E * 4
@@ -153,42 +154,37 @@ def tile_gatedcrossattention_pb_v_kernel(
         both = (nc.scalar.copy, nc.vector.tensor_copy)
 
         for c in range(PASSES):
-            regroup_hr(nc.vector.tensor_copy, c, slice(0, E))
-        quantise_hr(0)
+            regroup_hr(nc.vector.tensor_copy, c, slice(0, VECTOR_HR_COLS))
+            regroup_hr(nc.scalar.copy, c, slice(VECTOR_HR_COLS, E))
+        for c in range(PASSES):
+            quantise_hr(c)
 
-        def close(m):
-            quantise_dz(LAST, block_cols(m))
-            multiply(LAST, m)
+        def close(m, count=1):
+            quantise_dz(LAST, block_cols(m, count))
+            for i in range(count):
+                multiply(LAST, m + i)
 
+        square(0, 0)
+        square(LAST, 0)
         for q in range(CHUNKS):
             first = q * CHUNK_BLOCKS
             final = q == CHUNKS - 1
-            if q == 0:
-                square(0, q)
-                square(LAST, q)
-            for pair in (first, first + 2):
-                times_gate(0, block_cols(pair, 2))
+            times_gate(0, chunk_cols(q))
             if q > 0:
-                close(first - 1)
+                close(first - 2, 2)
                 store(first - 2, scalar_alone)
                 store(first - 1, scalar_alone)
             for pair in (first, first + 2):
                 dz_columns(0, block_cols(pair, 2))
             quantise_dz(0, block_cols(first, 2))
-            if q == 0:
-                quantise_hr(LAST)
-            else:
-                times_gate(LAST, block_cols(first, 2))
+            times_gate(LAST, block_cols(first, 2) if final else chunk_cols(q))
             quantise_dz(0, block_cols(first + 2, 2))
             for m in chunk_blocks(q):
                 multiply(0, m)
-            if q == 0:
-                times_gate(LAST, block_cols(first, 2))
-                times_gate(LAST, block_cols(first + 2, 2))
-            dz_columns(LAST, block_cols(first))
-            dz_columns(LAST, block_cols(first + 1))
-            close(first)
             if final:
+                dz_columns(LAST, block_cols(first))
+                dz_columns(LAST, block_cols(first + 1))
+                close(first)
                 times_gate(LAST, block_cols(first + 2, 2))
                 close(first + 1)
                 dz_columns(LAST, block_cols(first + 2))
@@ -200,10 +196,9 @@ def tile_gatedcrossattention_pb_v_kernel(
                 store(first + 2, both)
                 store(first + 3, both)
             else:
-                dz_columns(LAST, block_cols(first + 2))
-                close(first + 1)
-                dz_columns(LAST, block_cols(first + 3))
-                close(first + 2)
+                for pair in (first, first + 2):
+                    dz_columns(LAST, block_cols(pair, 2))
+                close(first, 2)
                 square(0, q + 1)
                 store(first, scalar_alone)
                 store(first + 1, scalar_alone)

@@ -59,6 +59,7 @@ def tile_gatedcrossattention_pb_v_kernel(
         g_raw = [keep.tile([P, PACK, E], BF16, name="g_raw%d" % c) for c in range(PASSES)]
         u_raw = [keep.tile([P, PACK, E], F32, name="u_raw%d" % c) for c in range(PASSES)]
         factor = [keep.tile([P, PACK, E], F32, name="factor%d" % c) for c in range(PASSES)]
+        gated = [keep.tile([P, PACK, E], F32, name="gated%d" % c) for c in range(PASSES)]
 
         for c in range(PASSES):
             nc.sync.dma_start(out=hr_raw[c][:], in_=pass_rows(hr, c))
@@ -101,7 +102,7 @@ def tile_gatedcrossattention_pb_v_kernel(
 
         def times_gate(c, cols):
             nc.vector.scalar_tensor_tensor(
-                out=factor[c][:, :, cols],
+                out=gated[c][:, :, cols],
                 in0=factor[c][:, :, cols],
                 scalar=1.0,
                 in1=u_raw[c][:, :, cols],
@@ -112,7 +113,7 @@ def tile_gatedcrossattention_pb_v_kernel(
         def dz_columns(c, cols):
             nc.vector.scalar_tensor_tensor(
                 out=dz_grouped[c][:, cols, :],
-                in0=factor[c][:, :, cols].rearrange("p j e -> p e j"),
+                in0=gated[c][:, :, cols].rearrange("p j e -> p e j"),
                 scalar=-1.0,
                 in1=g_raw[c][:, :, cols].rearrange("p j e -> p e j"),
                 op0=ALU.mult,

@@ -56,19 +56,23 @@ def tile_gatedcrossattention_pb_v_kernel(
         stack.enter_context(tc.manual_schedule())
 
         hr_raw = [keep.tile([P, PACK, E], BF16, name="hr_raw%d" % c) for c in range(PASSES)]
-        g_raw = [keep.tile([P, PACK, E], BF16, name="g_raw%d" % c) for c in range(PASSES)]
+        g_raw = [
+            [keep.tile([P, PACK, CHUNK_COLS], BF16, name="g_raw%d_%d" % (c, q)) for q in range(CHUNKS)]
+            for c in range(PASSES)
+        ]
         u_raw = [keep.tile([P, PACK, E], F32, name="u_raw%d" % c) for c in range(PASSES)]
         factor = [keep.tile([P, PACK, E], F32, name="factor%d" % c) for c in range(PASSES)]
-        gated = [keep.tile([P, PACK, E], F32, name="gated%d" % c) for c in range(PASSES)]
+        gated = {}
 
         for c in range(PASSES):
             nc.sync.dma_start(out=hr_raw[c][:], in_=pass_rows(hr, c))
         for q in range(CHUNKS):
             for c in range(PASSES):
-                for dst, src in ((factor[c], h), (u_raw[c], u), (g_raw[c], grad_out)):
+                for dst, src in ((factor[c], h), (u_raw[c], u)):
                     nc.sync.dma_start(
                         out=dst[:, :, chunk_cols(q)], in_=pass_rows(src, c)[:, :, chunk_cols(q)]
                     )
+                nc.sync.dma_start(out=g_raw[c][q][:], in_=pass_rows(grad_out, c)[:, :, chunk_cols(q)])
 
         hr_grouped = [
             keep.tile([P, E, PACK], BF16, name="hr_grouped%d" % c, align_bytes=64)
@@ -100,24 +104,31 @@ def tile_gatedcrossattention_pb_v_kernel(
             view = factor[c][:, :, chunk_cols(q)]
             nc.scalar.activation(out=view, in_=view, func=ACT.Square)
 
-        def times_gate(c, cols):
+        def times_gate(c, m, count):
+            cols = block_cols(m, count)
+            tile = keep.tile([P, PACK, count * M_TILE], F32, name="gated%d_%d" % (c, m))
             nc.vector.scalar_tensor_tensor(
-                out=gated[c][:, :, cols],
+                out=tile[:],
                 in0=factor[c][:, :, cols],
                 scalar=1.0,
                 in1=u_raw[c][:, :, cols],
                 op0=ALU.subtract,
                 op1=ALU.mult,
             )
+            for i in range(count):
+                gated[c, m + i] = (tile, i * M_TILE)
 
-        def dz_columns(c, cols):
-            nc.vector.scalar_tensor_tensor(
-                out=dz_grouped[c][:, cols, :],
-                in0=gated[c][:, :, cols].rearrange("p j e -> p e j"),
-                scalar=-1.0,
-                in1=g_raw[c][:, :, cols].rearrange("p j e -> p e j"),
-                op0=ALU.mult,
-                op1=ALU.mult,
+        def dz_columns(c, m, count=1):
+            tile, at = gated[c, m]
+            g_at = (m % CHUNK_BLOCKS) * M_TILE
+            width = count * M_TILE
+            nc.vector.tensor_tensor(
+                out=dz_grouped[c][:, block_cols(m, count), :].rearrange("p (b i) j -> p b j i", i=RUN),
+                in0=tile[:, :, at : at + width].rearrange("p j (b i) -> p b j i", i=RUN),
+                in1=g_raw[c][m // CHUNK_BLOCKS][:, :, g_at : g_at + width].rearrange(
+                    "p j (b i) -> p b j i", i=RUN
+                ),
+                op=ALU.mult,
             )
 
         def quantise_dz(c, cols):
@@ -151,8 +162,14 @@ def tile_gatedcrossattention_pb_v_kernel(
                 copies[n](out=results[m][:, n * N_TILE : (n + 1) * N_TILE], in_=sums[m, n][:])
             nc.sync.dma_start(out=out[block_cols(m), :], in_=results[m][:])
 
-        scalar_alone = (nc.scalar.copy, nc.scalar.copy)
-        both = (nc.scalar.copy, nc.vector.tensor_copy)
+        def by_scalar(out, in_):
+            nc.scalar.mul(out=out, in_=in_, mul=-1.0)
+
+        def by_vector(out, in_):
+            nc.vector.tensor_scalar_mul(out=out, in0=in_, scalar1=-1.0)
+
+        scalar_alone = (by_scalar, by_scalar)
+        both = (by_scalar, by_vector)
 
         for c in range(PASSES):
             regroup_hr(nc.vector.tensor_copy, c, slice(0, VECTOR_HR_COLS))
@@ -170,26 +187,26 @@ def tile_gatedcrossattention_pb_v_kernel(
         for q in range(CHUNKS):
             first = q * CHUNK_BLOCKS
             final = q == CHUNKS - 1
-            times_gate(0, chunk_cols(q))
+            times_gate(0, first, CHUNK_BLOCKS)
             if q > 0:
                 close(first - 2, 2)
                 store(first - 2, scalar_alone)
                 store(first - 1, scalar_alone)
             for pair in (first, first + 2):
-                dz_columns(0, block_cols(pair, 2))
+                dz_columns(0, pair, 2)
             quantise_dz(0, block_cols(first, 2))
-            times_gate(LAST, block_cols(first, 2) if final else chunk_cols(q))
+            times_gate(LAST, first, 2 if final else CHUNK_BLOCKS)
             quantise_dz(0, block_cols(first + 2, 2))
             for m in chunk_blocks(q):
                 multiply(0, m)
             if final:
-                dz_columns(LAST, block_cols(first))
-                dz_columns(LAST, block_cols(first + 1))
+                dz_columns(LAST, first)
+                dz_columns(LAST, first + 1)
                 close(first)
-                times_gate(LAST, block_cols(first + 2, 2))
+                times_gate(LAST, first + 2, 2)
                 close(first + 1)
-                dz_columns(LAST, block_cols(first + 2))
-                dz_columns(LAST, block_cols(first + 3))
+                dz_columns(LAST, first + 2)
+                dz_columns(LAST, first + 3)
                 close(first + 2)
                 close(first + 3)
                 store(first, scalar_alone)
@@ -198,7 +215,7 @@ def tile_gatedcrossattention_pb_v_kernel(
                 store(first + 3, both)
             else:
                 for pair in (first, first + 2):
-                    dz_columns(LAST, block_cols(pair, 2))
+                    dz_columns(LAST, pair, 2)
                 close(first, 2)
                 square(0, q + 1)
                 store(first, scalar_alone)

@@ -56,10 +56,8 @@ def tile_gatedcrossattention_pb_v_kernel(
         stack.enter_context(tc.manual_schedule())
 
         hr_raw = [keep.tile([P, PACK, E], BF16, name="hr_raw%d" % c) for c in range(PASSES)]
-        g_raw = [
-            [keep.tile([P, PACK, CHUNK_COLS], BF16, name="g_raw%d_%d" % (c, q)) for q in range(CHUNKS)]
-            for c in range(PASSES)
-        ]
+        g_first = keep.tile([P, PACK, E], BF16, name="g_first")
+        g_last = [keep.tile([P, PACK, CHUNK_COLS], BF16, name="g_last%d" % q) for q in range(CHUNKS)]
         u_raw = [keep.tile([P, PACK, E], F32, name="u_raw%d" % c) for c in range(PASSES)]
         factor = [keep.tile([P, PACK, E], F32, name="factor%d" % c) for c in range(PASSES)]
         gated = {}
@@ -72,7 +70,10 @@ def tile_gatedcrossattention_pb_v_kernel(
                     nc.sync.dma_start(
                         out=dst[:, :, chunk_cols(q)], in_=pass_rows(src, c)[:, :, chunk_cols(q)]
                     )
-                nc.sync.dma_start(out=g_raw[c][q][:], in_=pass_rows(grad_out, c)[:, :, chunk_cols(q)])
+                if c == LAST:
+                    nc.sync.dma_start(out=g_last[q][:], in_=pass_rows(grad_out, c)[:, :, chunk_cols(q)])
+                elif q == 0:
+                    nc.sync.dma_start(out=g_first[:], in_=pass_rows(grad_out, c))
 
         hr_grouped = [
             keep.tile([P, E, PACK], BF16, name="hr_grouped%d" % c, align_bytes=64)
@@ -120,12 +121,13 @@ def tile_gatedcrossattention_pb_v_kernel(
 
         def dz_columns(c, m, count=1):
             tile, at = gated[c, m]
-            g_at = (m % CHUNK_BLOCKS) * M_TILE
+            g_tile = g_last[m // CHUNK_BLOCKS] if c == LAST else g_first
+            g_at = (m % CHUNK_BLOCKS if c == LAST else m) * M_TILE
             width = count * M_TILE
             nc.vector.tensor_tensor(
                 out=dz_grouped[c][:, block_cols(m, count), :].rearrange("p (b i) j -> p b j i", i=RUN),
                 in0=tile[:, :, at : at + width].rearrange("p j (b i) -> p b j i", i=RUN),
-                in1=g_raw[c][m // CHUNK_BLOCKS][:, :, g_at : g_at + width].rearrange(
+                in1=g_tile[:, :, g_at : g_at + width].rearrange(
                     "p j (b i) -> p b j i", i=RUN
                 ),
                 op=ALU.mult,

@@ -26,6 +26,7 @@ CHUNK_BLOCKS = 4
 CHUNK_COLS = CHUNK_BLOCKS * M_TILE
 CHUNKS = E // CHUNK_COLS
 RUN = 4
+ROW_PAIRS = (slice(0, 2), slice(2, 4))
 VECTOR_HR_COLS = 704
 
 FLOPS = 2 * TOKENS * E * E
@@ -64,16 +65,16 @@ def tile_gatedcrossattention_pb_v_kernel(
 
         for c in range(PASSES):
             nc.sync.dma_start(out=hr_raw[c][:], in_=pass_rows(hr, c))
+        for rows in ROW_PAIRS:
+            for dst, src in ((factor[0], h), (u_raw[0], u)):
+                nc.sync.dma_start(out=dst[:, rows, :], in_=pass_rows(src, 0)[:, rows, :])
+        nc.sync.dma_start(out=g_first[:], in_=pass_rows(grad_out, 0))
         for q in range(CHUNKS):
-            for c in range(PASSES):
-                for dst, src in ((factor[c], h), (u_raw[c], u)):
-                    nc.sync.dma_start(
-                        out=dst[:, :, chunk_cols(q)], in_=pass_rows(src, c)[:, :, chunk_cols(q)]
-                    )
-                if c == LAST:
-                    nc.sync.dma_start(out=g_last[q][:], in_=pass_rows(grad_out, c)[:, :, chunk_cols(q)])
-                elif q == 0:
-                    nc.sync.dma_start(out=g_first[:], in_=pass_rows(grad_out, c))
+            for dst, src in ((factor[LAST], h), (u_raw[LAST], u)):
+                nc.sync.dma_start(
+                    out=dst[:, :, chunk_cols(q)], in_=pass_rows(src, LAST)[:, :, chunk_cols(q)]
+                )
+            nc.sync.dma_start(out=g_last[q][:], in_=pass_rows(grad_out, LAST)[:, :, chunk_cols(q)])
 
         hr_grouped = [
             keep.tile([P, E, PACK], BF16, name="hr_grouped%d" % c, align_bytes=64)
@@ -101,9 +102,22 @@ def tile_gatedcrossattention_pb_v_kernel(
                 in_=hr_grouped[c][:].rearrange("p e j -> p (e j)"),
             )
 
-        def square(c, q):
-            view = factor[c][:, :, chunk_cols(q)]
+        def square(view):
             nc.scalar.activation(out=view, in_=view, func=ACT.Square)
+
+        gated_first = keep.tile([P, PACK, E], F32, name="gated_first")
+        for m in range(E // M_TILE):
+            gated[0, m] = (gated_first, m * M_TILE)
+
+        def times_gate_rows(rows):
+            nc.vector.scalar_tensor_tensor(
+                out=gated_first[:, rows, :],
+                in0=factor[0][:, rows, :],
+                scalar=1.0,
+                in1=u_raw[0][:, rows, :],
+                op0=ALU.subtract,
+                op1=ALU.mult,
+            )
 
         def times_gate(c, m, count):
             cols = block_cols(m, count)
@@ -184,42 +198,46 @@ def tile_gatedcrossattention_pb_v_kernel(
             for i in range(count):
                 multiply(LAST, m + i)
 
-        square(0, 0)
-        square(LAST, 0)
+        for rows in ROW_PAIRS:
+            square(factor[0][:, rows, :])
+        square(factor[LAST][:, :, chunk_cols(0)])
+        for rows in ROW_PAIRS:
+            times_gate_rows(rows)
+        pairs = range(0, E // M_TILE, 2)
+        for pair in pairs:
+            dz_columns(0, pair, 2)
+        for pair in pairs:
+            quantise_dz(0, block_cols(pair, 2))
+        for m in chunk_blocks(0):
+            multiply(0, m)
+
         for q in range(CHUNKS):
             first = q * CHUNK_BLOCKS
             final = q == CHUNKS - 1
-            times_gate(0, first, CHUNK_BLOCKS)
-            if q > 0:
-                close(first - 2, 2)
-                store(first - 2, scalar_alone)
-                store(first - 1, scalar_alone)
-            for pair in (first, first + 2):
-                dz_columns(0, pair, 2)
-            quantise_dz(0, block_cols(first, 2))
-            times_gate(LAST, first, 2 if final else CHUNK_BLOCKS)
-            quantise_dz(0, block_cols(first + 2, 2))
-            for m in chunk_blocks(q):
-                multiply(0, m)
+
+            def finish(m):
+                if final:
+                    multiply(0, m)
+                close(m)
+
+            times_gate(LAST, first, 2)
+            dz_columns(LAST, first)
+            dz_columns(LAST, first + 1)
+            finish(first)
+            times_gate(LAST, first + 2, 2)
+            finish(first + 1)
+            dz_columns(LAST, first + 2)
+            dz_columns(LAST, first + 3)
+            finish(first + 2)
+            finish(first + 3)
             if final:
-                dz_columns(LAST, first)
-                dz_columns(LAST, first + 1)
-                close(first)
-                times_gate(LAST, first + 2, 2)
-                close(first + 1)
-                dz_columns(LAST, first + 2)
-                dz_columns(LAST, first + 3)
-                close(first + 2)
-                close(first + 3)
                 store(first, scalar_alone)
                 store(first + 1, scalar_alone)
                 store(first + 2, both)
                 store(first + 3, both)
             else:
-                for pair in (first, first + 2):
-                    dz_columns(LAST, pair, 2)
-                close(first, 2)
-                square(0, q + 1)
+                square(factor[LAST][:, :, block_cols(first + CHUNK_BLOCKS, 2)])
                 store(first, scalar_alone)
-                store(first + 1, scalar_alone)
-                square(LAST, q + 1)
+                square(factor[LAST][:, :, block_cols(first + CHUNK_BLOCKS + 2, 2)])
+                for m in (first + 1, first + 2, first + 3):
+                    store(m, scalar_alone)

@@ -22,12 +22,12 @@ M_TILE = 128
 N_TILE = 512
 N_BLOCKS = E // N_TILE
 PSUM_BANKS = 8
-CHUNK_BLOCKS = 4
-CHUNK_COLS = CHUNK_BLOCKS * M_TILE
-CHUNKS = E // CHUNK_COLS
+HALF_BLOCKS = 4
+HALF_COLS = HALF_BLOCKS * M_TILE
+HALVES = E // HALF_COLS
 RUN = 4
 ROW_PAIRS = (slice(0, 2), slice(2, 4))
-VECTOR_HR_COLS = 704
+VECTOR_HR_COLS = (256, 512)
 
 FLOPS = 2 * TOKENS * E * E
 BYTES = TOKENS * E * (2 + 2 + 4 + 4) + E * E * 4
@@ -42,14 +42,11 @@ def tile_gatedcrossattention_pb_v_kernel(
         flat = dram.flatten_outer_dims()
         return flat[c * K_PASS : (c + 1) * K_PASS, :].rearrange("(p j) e -> p j e", j=PACK)
 
-    def chunk_cols(q):
-        return slice(q * CHUNK_COLS, (q + 1) * CHUNK_COLS)
+    def half_cols(q):
+        return slice(q * HALF_COLS, (q + 1) * HALF_COLS)
 
     def block_cols(m, count=1):
         return slice(m * M_TILE, (m + count) * M_TILE)
-
-    def chunk_blocks(q):
-        return range(q * CHUNK_BLOCKS, (q + 1) * CHUNK_BLOCKS)
 
     with ExitStack() as stack:
         keep = stack.enter_context(tc.tile_pool(name="keep", bufs=1))
@@ -57,24 +54,32 @@ def tile_gatedcrossattention_pb_v_kernel(
         stack.enter_context(tc.manual_schedule())
 
         hr_raw = [keep.tile([P, PACK, E], BF16, name="hr_raw%d" % c) for c in range(PASSES)]
-        g_first = keep.tile([P, PACK, E], BF16, name="g_first")
-        g_last = [keep.tile([P, PACK, CHUNK_COLS], BF16, name="g_last%d" % q) for q in range(CHUNKS)]
-        u_raw = [keep.tile([P, PACK, E], F32, name="u_raw%d" % c) for c in range(PASSES)]
+        g_raw = [keep.tile([P, PACK, E], BF16, name="g_raw%d" % c) for c in range(PASSES)]
         factor = [keep.tile([P, PACK, E], F32, name="factor%d" % c) for c in range(PASSES)]
-        gated = {}
+        u_raw = [
+            [keep.tile([P, PACK, HALF_COLS], F32, name="u_raw%d_%d" % (c, q)) for q in range(HALVES)]
+            for c in range(PASSES)
+        ]
 
-        for c in range(PASSES):
+        def load_rows(c):
+            for rows in ROW_PAIRS:
+                nc.sync.dma_start(out=factor[c][:, rows, :], in_=pass_rows(h, c)[:, rows, :])
+                nc.sync.dma_start(out=g_raw[c][:, rows, :], in_=pass_rows(grad_out, c)[:, rows, :])
+
+        def load_hr(c):
             nc.sync.dma_start(out=hr_raw[c][:], in_=pass_rows(hr, c))
-        for rows in ROW_PAIRS:
-            for dst, src in ((factor[0], h), (u_raw[0], u)):
-                nc.sync.dma_start(out=dst[:, rows, :], in_=pass_rows(src, 0)[:, rows, :])
-        nc.sync.dma_start(out=g_first[:], in_=pass_rows(grad_out, 0))
-        for q in range(CHUNKS):
-            for dst, src in ((factor[LAST], h), (u_raw[LAST], u)):
-                nc.sync.dma_start(
-                    out=dst[:, :, chunk_cols(q)], in_=pass_rows(src, LAST)[:, :, chunk_cols(q)]
-                )
-            nc.sync.dma_start(out=g_last[q][:], in_=pass_rows(grad_out, LAST)[:, :, chunk_cols(q)])
+
+        def load_u(c, q):
+            nc.sync.dma_start(out=u_raw[c][q][:], in_=pass_rows(u, c)[:, :, half_cols(q)])
+
+        load_rows(0)
+        load_hr(0)
+        load_u(0, 0)
+        load_hr(LAST)
+        load_rows(LAST)
+        load_u(LAST, 0)
+        load_u(0, 1)
+        load_u(LAST, 1)
 
         hr_grouped = [
             keep.tile([P, E, PACK], BF16, name="hr_grouped%d" % c, align_bytes=64)
@@ -95,6 +100,12 @@ def tile_gatedcrossattention_pb_v_kernel(
                 in_=hr_raw[c][:, :, cols].rearrange("p j (b i) -> p b j i", i=RUN),
             )
 
+        def regroup_by_vector(c):
+            regroup_hr(nc.vector.tensor_copy, c, slice(0, VECTOR_HR_COLS[c]))
+
+        def regroup_by_scalar(c):
+            regroup_hr(nc.scalar.copy, c, slice(VECTOR_HR_COLS[c], E))
+
         def quantise_hr(c):
             nc.vector.quantize_mx(
                 out=hr_codes[:, c, :].bitcast(E4M3_X4),
@@ -102,52 +113,35 @@ def tile_gatedcrossattention_pb_v_kernel(
                 in_=hr_grouped[c][:].rearrange("p e j -> p (e j)"),
             )
 
-        def square(view):
+        def square(c, rows):
+            view = factor[c][:, rows, :]
             nc.scalar.activation(out=view, in_=view, func=ACT.Square)
 
-        gated_first = keep.tile([P, PACK, E], F32, name="gated_first")
-        for m in range(E // M_TILE):
-            gated[0, m] = (gated_first, m * M_TILE)
-
-        def times_gate_rows(rows):
+        def times_gradient(c, rows):
+            view = factor[c][:, rows, :]
             nc.vector.scalar_tensor_tensor(
-                out=gated_first[:, rows, :],
-                in0=factor[0][:, rows, :],
+                out=view,
+                in0=view,
                 scalar=1.0,
-                in1=u_raw[0][:, rows, :],
+                in1=g_raw[c][:, rows, :],
                 op0=ALU.subtract,
                 op1=ALU.mult,
             )
-
-        def times_gate(c, m, count):
-            cols = block_cols(m, count)
-            tile = keep.tile([P, PACK, count * M_TILE], F32, name="gated%d_%d" % (c, m))
-            nc.vector.scalar_tensor_tensor(
-                out=tile[:],
-                in0=factor[c][:, :, cols],
-                scalar=1.0,
-                in1=u_raw[c][:, :, cols],
-                op0=ALU.subtract,
-                op1=ALU.mult,
-            )
-            for i in range(count):
-                gated[c, m + i] = (tile, i * M_TILE)
 
         def dz_columns(c, m, count=1):
-            tile, at = gated[c, m]
-            g_tile = g_last[m // CHUNK_BLOCKS] if c == LAST else g_first
-            g_at = (m % CHUNK_BLOCKS if c == LAST else m) * M_TILE
-            width = count * M_TILE
+            u_at = (m % HALF_BLOCKS) * M_TILE
+            u_cols = slice(u_at, u_at + count * M_TILE)
             nc.vector.tensor_tensor(
                 out=dz_grouped[c][:, block_cols(m, count), :].rearrange("p (b i) j -> p b j i", i=RUN),
-                in0=tile[:, :, at : at + width].rearrange("p j (b i) -> p b j i", i=RUN),
-                in1=g_tile[:, :, g_at : g_at + width].rearrange(
+                in0=factor[c][:, :, block_cols(m, count)].rearrange("p j (b i) -> p b j i", i=RUN),
+                in1=u_raw[c][m // HALF_BLOCKS][:, :, u_cols].rearrange(
                     "p j (b i) -> p b j i", i=RUN
                 ),
                 op=ALU.mult,
             )
 
-        def quantise_dz(c, cols):
+        def quantise_dz(c, m, count=1):
+            cols = block_cols(m, count)
             nc.vector.quantize_mx(
                 out=dz_codes[:, c, cols].bitcast(E5M2_X4),
                 scales=dz_scales[:, c, cols],
@@ -172,12 +166,6 @@ def tile_gatedcrossattention_pb_v_kernel(
                     stop=(c == LAST),
                 )
 
-        def store(m, copies):
-            results[m] = keep.tile([M_TILE, E], F32, name="result%d" % m)
-            for n in range(N_BLOCKS):
-                copies[n](out=results[m][:, n * N_TILE : (n + 1) * N_TILE], in_=sums[m, n][:])
-            nc.sync.dma_start(out=out[block_cols(m), :], in_=results[m][:])
-
         def by_scalar(out, in_):
             nc.scalar.mul(out=out, in_=in_, mul=-1.0)
 
@@ -187,57 +175,56 @@ def tile_gatedcrossattention_pb_v_kernel(
         scalar_alone = (by_scalar, by_scalar)
         both = (by_scalar, by_vector)
 
-        for c in range(PASSES):
-            regroup_hr(nc.vector.tensor_copy, c, slice(0, VECTOR_HR_COLS))
-            regroup_hr(nc.scalar.copy, c, slice(VECTOR_HR_COLS, E))
-        for c in range(PASSES):
-            quantise_hr(c)
+        def store(m, copies):
+            results[m] = keep.tile([M_TILE, E], F32, name="result%d" % m)
+            for n in range(N_BLOCKS):
+                copies[n](out=results[m][:, n * N_TILE : (n + 1) * N_TILE], in_=sums[m, n][:])
+            nc.sync.dma_start(out=out[block_cols(m), :], in_=results[m][:])
 
-        def close(m, count=1):
-            quantise_dz(LAST, block_cols(m, count))
-            for i in range(count):
-                multiply(LAST, m + i)
-
-        for rows in ROW_PAIRS:
-            square(factor[0][:, rows, :])
-        square(factor[LAST][:, :, chunk_cols(0)])
-        for rows in ROW_PAIRS:
-            times_gate_rows(rows)
-        pairs = range(0, E // M_TILE, 2)
-        for pair in pairs:
-            dz_columns(0, pair, 2)
-        for pair in pairs:
-            quantise_dz(0, block_cols(pair, 2))
-        for m in chunk_blocks(0):
+        for j in range(PACK):
+            square(0, slice(j, j + 1))
+            times_gradient(0, slice(j, j + 1))
+        regroup_by_vector(0)
+        regroup_by_scalar(0)
+        dz_columns(0, 0, 2)
+        quantise_hr(0)
+        dz_columns(0, 2, 2)
+        quantise_dz(0, 0, 2)
+        quantise_dz(0, 2, 2)
+        for m in range(HALF_BLOCKS):
             multiply(0, m)
 
-        for q in range(CHUNKS):
-            first = q * CHUNK_BLOCKS
-            final = q == CHUNKS - 1
+        regroup_by_vector(LAST)
+        regroup_by_scalar(LAST)
+        quantise_hr(LAST)
+        for j in range(PACK):
+            square(LAST, slice(j, j + 1))
+            times_gradient(LAST, slice(j, j + 1))
 
-            def finish(m):
-                if final:
-                    multiply(0, m)
-                close(m)
+        def close(m):
+            quantise_dz(LAST, m)
+            multiply(LAST, m)
 
-            times_gate(LAST, first, 2)
-            dz_columns(LAST, first)
-            dz_columns(LAST, first + 1)
-            finish(first)
-            times_gate(LAST, first + 2, 2)
-            finish(first + 1)
-            dz_columns(LAST, first + 2)
-            dz_columns(LAST, first + 3)
-            finish(first + 2)
-            finish(first + 3)
-            if final:
-                store(first, scalar_alone)
-                store(first + 1, scalar_alone)
-                store(first + 2, both)
-                store(first + 3, both)
-            else:
-                square(factor[LAST][:, :, block_cols(first + CHUNK_BLOCKS, 2)])
-                store(first, scalar_alone)
-                square(factor[LAST][:, :, block_cols(first + CHUNK_BLOCKS + 2, 2)])
-                for m in (first + 1, first + 2, first + 3):
-                    store(m, scalar_alone)
+        dz_columns(LAST, 0)
+        dz_columns(LAST, 1)
+        close(0)
+        close(1)
+        store(0, scalar_alone)
+        dz_columns(LAST, 2)
+        dz_columns(LAST, 3)
+        close(2)
+        close(3)
+        for m in (1, 2, 3):
+            store(m, scalar_alone)
+
+        for m in (4, 6):
+            dz_columns(0, m, 2)
+            quantise_dz(0, m, 2)
+            multiply(0, m)
+            dz_columns(LAST, m)
+            close(m)
+            store(m, scalar_alone)
+            multiply(0, m + 1)
+            dz_columns(LAST, m + 1)
+            close(m + 1)
+            store(m + 1, both if m == 6 else scalar_alone)

@@ -27,7 +27,7 @@ HALF_COLS = HALF_BLOCKS * M_TILE
 HALVES = E // HALF_COLS
 RUN = 4
 ROW_PAIRS = (slice(0, 2), slice(2, 4))
-VECTOR_HR_COLS = (256, 512)
+VECTOR_HR_COLS = 512
 
 FLOPS = 2 * TOKENS * E * E
 BYTES = TOKENS * E * (2 + 2 + 4 + 4) + E * E * 4
@@ -72,8 +72,8 @@ def tile_gatedcrossattention_pb_v_kernel(
         def load_u(c, q):
             nc.sync.dma_start(out=u_raw[c][q][:], in_=pass_rows(u, c)[:, :, half_cols(q)])
 
-        load_rows(0)
         load_hr(0)
+        load_rows(0)
         load_u(0, 0)
         load_hr(LAST)
         load_rows(LAST)
@@ -99,12 +99,6 @@ def tile_gatedcrossattention_pb_v_kernel(
                 out=hr_grouped[c][:, cols, :].rearrange("p (b i) j -> p b j i", i=RUN),
                 in_=hr_raw[c][:, :, cols].rearrange("p j (b i) -> p b j i", i=RUN),
             )
-
-        def regroup_by_vector(c):
-            regroup_hr(nc.vector.tensor_copy, c, slice(0, VECTOR_HR_COLS[c]))
-
-        def regroup_by_scalar(c):
-            regroup_hr(nc.scalar.copy, c, slice(VECTOR_HR_COLS[c], E))
 
         def quantise_hr(c):
             nc.vector.quantize_mx(
@@ -181,50 +175,60 @@ def tile_gatedcrossattention_pb_v_kernel(
                 copies[n](out=results[m][:, n * N_TILE : (n + 1) * N_TILE], in_=sums[m, n][:])
             nc.sync.dma_start(out=out[block_cols(m), :], in_=results[m][:])
 
-        for j in range(PACK):
-            square(0, slice(j, j + 1))
-            times_gradient(0, slice(j, j + 1))
-        regroup_by_vector(0)
-        regroup_by_scalar(0)
-        dz_columns(0, 0, 2)
-        quantise_hr(0)
-        dz_columns(0, 2, 2)
-        quantise_dz(0, 0, 2)
-        quantise_dz(0, 2, 2)
-        for m in range(HALF_BLOCKS):
-            multiply(0, m)
-
-        regroup_by_vector(LAST)
-        regroup_by_scalar(LAST)
-        quantise_hr(LAST)
-        for j in range(PACK):
-            square(LAST, slice(j, j + 1))
-            times_gradient(LAST, slice(j, j + 1))
-
         def close(m):
             quantise_dz(LAST, m)
             multiply(LAST, m)
 
+        def first_products(c):
+            for j in range(PACK):
+                square(c, slice(j, j + 1))
+                times_gradient(c, slice(j, j + 1))
+
+        regroup_hr(nc.vector.tensor_copy, 0, slice(0, E))
+        quantise_hr(0)
+
+        first_products(0)
+        dz_columns(0, 0, 2)
+        dz_columns(0, 2, 2)
+        quantise_dz(0, 0, 2)
+        regroup_hr(nc.vector.tensor_copy, LAST, slice(0, VECTOR_HR_COLS))
+        regroup_hr(nc.scalar.copy, LAST, slice(VECTOR_HR_COLS, E))
+        quantise_dz(0, 2, 2)
+        for m in range(HALF_BLOCKS):
+            multiply(0, m)
+        quantise_hr(LAST)
+
+        first_products(LAST)
         dz_columns(LAST, 0)
         dz_columns(LAST, 1)
         close(0)
-        close(1)
         store(0, scalar_alone)
         dz_columns(LAST, 2)
+        close(1)
+        store(1, scalar_alone)
         dz_columns(LAST, 3)
         close(2)
-        close(3)
-        for m in (1, 2, 3):
-            store(m, scalar_alone)
+        store(2, scalar_alone)
 
-        for m in (4, 6):
-            dz_columns(0, m, 2)
-            quantise_dz(0, m, 2)
+        dz_columns(0, 4, 2)
+        close(3)
+        store(3, scalar_alone)
+        dz_columns(LAST, 4)
+        quantise_dz(0, 4, 2)
+        for m in (4, 5):
             multiply(0, m)
-            dz_columns(LAST, m)
-            close(m)
-            store(m, scalar_alone)
-            multiply(0, m + 1)
-            dz_columns(LAST, m + 1)
-            close(m + 1)
-            store(m + 1, both if m == 6 else scalar_alone)
+        dz_columns(LAST, 5)
+        close(4)
+        store(4, scalar_alone)
+        dz_columns(0, 6, 2)
+        close(5)
+        store(5, scalar_alone)
+        dz_columns(LAST, 6)
+        quantise_dz(0, 6, 2)
+        for m in (6, 7):
+            multiply(0, m)
+        dz_columns(LAST, 7)
+        close(6)
+        close(7)
+        store(6, both)
+        store(7, both)

@@ -179,26 +179,29 @@ def tile_gatedcrossattention_pb_v_kernel(
             quantise_dz(LAST, m)
             multiply(LAST, m)
 
-        def first_products(c):
-            for j in range(PACK):
+        def first_products(c, token_rows):
+            for j in token_rows:
                 square(c, slice(j, j + 1))
                 times_gradient(c, slice(j, j + 1))
 
         regroup_hr(nc.vector.tensor_copy, 0, slice(0, E))
         quantise_hr(0)
 
-        first_products(0)
+        first_products(0, range(PACK))
         dz_columns(0, 0, 2)
         dz_columns(0, 2, 2)
         quantise_dz(0, 0, 2)
         regroup_hr(nc.vector.tensor_copy, LAST, slice(0, VECTOR_HR_COLS))
         regroup_hr(nc.scalar.copy, LAST, slice(VECTOR_HR_COLS, E))
-        quantise_dz(0, 2, 2)
-        for m in range(HALF_BLOCKS):
+        for m in (0, 1):
             multiply(0, m)
         quantise_hr(LAST)
 
-        first_products(LAST)
+        first_products(LAST, (0, 1))
+        quantise_dz(0, 2, 2)
+        for m in (2, 3):
+            multiply(0, m)
+        first_products(LAST, (2, 3))
         dz_columns(LAST, 0)
         dz_columns(LAST, 1)
         close(0)
@@ -213,22 +216,22 @@ def tile_gatedcrossattention_pb_v_kernel(
         dz_columns(0, 4, 2)
         close(3)
         store(3, scalar_alone)
-        dz_columns(LAST, 4)
         quantise_dz(0, 4, 2)
-        for m in (4, 5):
-            multiply(0, m)
+        multiply(0, 4)
+        dz_columns(LAST, 4)
         dz_columns(LAST, 5)
         close(4)
         store(4, scalar_alone)
+        multiply(0, 5)
         dz_columns(0, 6, 2)
         close(5)
         store(5, scalar_alone)
         dz_columns(LAST, 6)
         quantise_dz(0, 6, 2)
-        for m in (6, 7):
-            multiply(0, m)
+        multiply(0, 6)
         dz_columns(LAST, 7)
         close(6)
+        multiply(0, 7)
         close(7)
         store(6, both)
         store(7, both)

@@ -223,15 +223,17 @@ def tile_gatedcrossattention_pb_v_kernel(
         close(4)
         store(4, scalar_alone)
         multiply(0, 5)
-        dz_columns(0, 6, 2)
+        dz_columns(0, 6)
         close(5)
         store(5, scalar_alone)
         dz_columns(LAST, 6)
-        quantise_dz(0, 6, 2)
+        quantise_dz(0, 6)
         multiply(0, 6)
-        dz_columns(LAST, 7)
+        dz_columns(0, 7)
         close(6)
+        store(6, scalar_alone)
+        dz_columns(LAST, 7)
+        quantise_dz(0, 7)
         multiply(0, 7)
         close(7)
-        store(6, both)
         store(7, both)

@@ -190,16 +190,13 @@ def tile_gatedcrossattention_pb_v_kernel(
         first_products(0, range(PACK))
         dz_columns(0, 0, 2)
         dz_columns(0, 2, 2)
-        quantise_dz(0, 0, 2)
         regroup_hr(nc.vector.tensor_copy, LAST, slice(0, VECTOR_HR_COLS))
         regroup_hr(nc.scalar.copy, LAST, slice(VECTOR_HR_COLS, E))
-        for m in (0, 1):
-            multiply(0, m)
         quantise_hr(LAST)
 
         first_products(LAST, (0, 1))
-        quantise_dz(0, 2, 2)
-        for m in (2, 3):
+        quantise_dz(0, 0, HALF_BLOCKS)
+        for m in range(HALF_BLOCKS):
             multiply(0, m)
         first_products(LAST, (2, 3))
         dz_columns(LAST, 0)

from contextlib import ExitStack

import concourse.mybir as mybir

F32 = mybir.dt.float32
BF16 = mybir.dt.bfloat16
U32 = mybir.dt.uint32
U8 = mybir.dt.uint8
E4M3_X4 = mybir.dt.float8_e4m3fn_x4
E5M2_X4 = mybir.dt.float8_e5m2_x4
ALU = mybir.AluOpType
ACT = mybir.ActivationFunctionType

P = 128
PACK = 4
K_PASS = P * PACK
TOKENS = 1024
E = 1024
PASSES = TOKENS // K_PASS
LAST = PASSES - 1
M_TILE = 128
N_TILE = 512
N_BLOCKS = E // N_TILE
PSUM_BANKS = 8
HALF_BLOCKS = 4
HALF_COLS = HALF_BLOCKS * M_TILE
HALVES = E // HALF_COLS
RUN = 4
ROW_PAIRS = (slice(0, 2), slice(2, 4))
VECTOR_HR_COLS = 512

FLOPS = 2 * TOKENS * E * E
BYTES = TOKENS * E * (2 + 2 + 4 + 4) + E * E * 4


def tile_gatedcrossattention_pb_v_kernel(
    tc, query, hr, Wu, bu, Wh, bh, u, h, grad_out, out
):
    nc = tc.nc

    def pass_rows(dram, c):
        flat = dram.flatten_outer_dims()
        return flat[c * K_PASS : (c + 1) * K_PASS, :].rearrange("(p j) e -> p j e", j=PACK)

    def half_cols(q):
        return slice(q * HALF_COLS, (q + 1) * HALF_COLS)

    def block_cols(m, count=1):
        return slice(m * M_TILE, (m + count) * M_TILE)

    with ExitStack() as stack:
        keep = stack.enter_context(tc.tile_pool(name="keep", bufs=1))
        psum = stack.enter_context(tc.psum_pool(name="psum", bufs=PSUM_BANKS))
        stack.enter_context(tc.manual_schedule())

        hr_raw = [keep.tile([P, PACK, E], BF16, name="hr_raw%d" % c) for c in range(PASSES)]
        g_raw = [keep.tile([P, PACK, E], BF16, name="g_raw%d" % c) for c in range(PASSES)]
        factor = [keep.tile([P, PACK, E], F32, name="factor%d" % c) for c in range(PASSES)]
        u_raw = [
            [keep.tile([P, PACK, HALF_COLS], F32, name="u_raw%d_%d" % (c, q)) for q in range(HALVES)]
            for c in range(PASSES)
        ]

        def load_rows(c):
            for rows in ROW_PAIRS:
                nc.sync.dma_start(out=factor[c][:, rows, :], in_=pass_rows(h, c)[:, rows, :])
                nc.sync.dma_start(out=g_raw[c][:, rows, :], in_=pass_rows(grad_out, c)[:, rows, :])

        def load_hr(c):
            nc.sync.dma_start(out=hr_raw[c][:], in_=pass_rows(hr, c))

        def load_u(c, q):
            nc.sync.dma_start(out=u_raw[c][q][:], in_=pass_rows(u, c)[:, :, half_cols(q)])

        load_hr(0)
        load_rows(0)
        load_u(0, 0)
        load_hr(LAST)
        load_rows(LAST)
        load_u(LAST, 0)
        load_u(0, 1)
        load_u(LAST, 1)

        hr_grouped = [
            keep.tile([P, E, PACK], BF16, name="hr_grouped%d" % c, align_bytes=64)
            for c in range(PASSES)
        ]
        dz_grouped = [
            keep.tile([P, E, PACK], BF16, name="dz_grouped%d" % c, align_bytes=64)
            for c in range(PASSES)
        ]
        hr_codes = keep.tile([P, PASSES, E], U32, name="hr_codes", align_bytes=64)
        hr_scales = keep.tile([P, PASSES, E], U8, name="hr_scales", align_bytes=64)
        dz_codes = keep.tile([P, PASSES, E], U32, name="dz_codes", align_bytes=64)
        dz_scales = keep.tile([P, PASSES, E], U8, name="dz_scales", align_bytes=64)

        def regroup_hr(copy, c, cols):
            copy(
                out=hr_grouped[c][:, cols, :].rearrange("p (b i) j -> p b j i", i=RUN),
                in_=hr_raw[c][:, :, cols].rearrange("p j (b i) -> p b j i", i=RUN),
            )

        def quantise_hr(c):
            nc.vector.quantize_mx(
                out=hr_codes[:, c, :].bitcast(E4M3_X4),
                scales=hr_scales[:, c, :],
                in_=hr_grouped[c][:].rearrange("p e j -> p (e j)"),
            )

        def square(c, rows):
            view = factor[c][:, rows, :]
            nc.scalar.activation(out=view, in_=view, func=ACT.Square)

        def times_gradient(c, rows):
            view = factor[c][:, rows, :]
            nc.vector.scalar_tensor_tensor(
                out=view,
                in0=view,
                scalar=1.0,
                in1=g_raw[c][:, rows, :],
                op0=ALU.subtract,
                op1=ALU.mult,
            )

        def dz_columns(c, m, count=1):
            u_at = (m % HALF_BLOCKS) * M_TILE
            u_cols = slice(u_at, u_at + count * M_TILE)
            nc.vector.tensor_tensor(
                out=dz_grouped[c][:, block_cols(m, count), :].rearrange("p (b i) j -> p b j i", i=RUN),
                in0=factor[c][:, :, block_cols(m, count)].rearrange("p j (b i) -> p b j i", i=RUN),
                in1=u_raw[c][m // HALF_BLOCKS][:, :, u_cols].rearrange(
                    "p j (b i) -> p b j i", i=RUN
                ),
                op=ALU.mult,
            )

        def quantise_dz(c, m, count=1):
            cols = block_cols(m, count)
            nc.vector.quantize_mx(
                out=dz_codes[:, c, cols].bitcast(E5M2_X4),
                scales=dz_scales[:, c, cols],
                in_=dz_grouped[c][:, cols, :].rearrange("p e j -> p (e j)"),
            )

        sums = {}
        results = {}

        def multiply(c, m):
            for n in range(N_BLOCKS):
                n_cols = slice(n * N_TILE, (n + 1) * N_TILE)
                if c == 0:
                    sums[m, n] = psum.tile([M_TILE, N_TILE], F32, name="sums")
                nc.tensor.matmul_mx(
                    out=sums[m, n][:],
                    lhsT=dz_codes[:, c, block_cols(m)].bitcast(E5M2_X4),
                    lhsT_scale=dz_scales[:, c, block_cols(m)],
                    rhs=hr_codes[:, c, n_cols].bitcast(E4M3_X4),
                    rhs_scale=hr_scales[:, c, n_cols],
                    start=(c == 0),
                    stop=(c == LAST),
                )

        def by_scalar(out, in_):
            nc.scalar.mul(out=out, in_=in_, mul=-1.0)

        def by_vector(out, in_):
            nc.vector.tensor_scalar_mul(out=out, in0=in_, scalar1=-1.0)

        scalar_alone = (by_scalar, by_scalar)
        both = (by_scalar, by_vector)

        def store(m, copies):
            results[m] = keep.tile([M_TILE, E], F32, name="result%d" % m)
            for n in range(N_BLOCKS):
                copies[n](out=results[m][:, n * N_TILE : (n + 1) * N_TILE], in_=sums[m, n][:])
            nc.sync.dma_start(out=out[block_cols(m), :], in_=results[m][:])

        def close(m):
            quantise_dz(LAST, m)
            multiply(LAST, m)

        def first_products(c, token_rows):
            for j in token_rows:
                square(c, slice(j, j + 1))
                times_gradient(c, slice(j, j + 1))

        regroup_hr(nc.vector.tensor_copy, 0, slice(0, E))
        quantise_hr(0)

        first_products(0, range(PACK))
        dz_columns(0, 0, 2)
        dz_columns(0, 2, 2)
        regroup_hr(nc.vector.tensor_copy, LAST, slice(0, VECTOR_HR_COLS))
        regroup_hr(nc.scalar.copy, LAST, slice(VECTOR_HR_COLS, E))
        quantise_hr(LAST)

        first_products(LAST, (0, 1))
        quantise_dz(0, 0, HALF_BLOCKS)
        for m in range(HALF_BLOCKS):
            multiply(0, m)
        first_products(LAST, (2, 3))
        dz_columns(LAST, 0)
        dz_columns(LAST, 1)
        close(0)
        store(0, scalar_alone)
        dz_columns(LAST, 2)
        close(1)
        store(1, scalar_alone)
        dz_columns(LAST, 3)
        close(2)
        store(2, scalar_alone)

        dz_columns(0, 4, 2)
        close(3)
        store(3, scalar_alone)
        quantise_dz(0, 4, 2)
        multiply(0, 4)
        dz_columns(LAST, 4)
        dz_columns(LAST, 5)
        close(4)
        store(4, scalar_alone)
        multiply(0, 5)
        dz_columns(0, 6)
        close(5)
        store(5, scalar_alone)
        dz_columns(LAST, 6)
        quantise_dz(0, 6)
        multiply(0, 6)
        dz_columns(0, 7)
        close(6)
        store(6, scalar_alone)
        dz_columns(LAST, 7)
        quantise_dz(0, 7)
        multiply(0, 7)
        close(7)
        store(7, both)
